import numpy as np
import ml_dtypes

BF16 = ml_dtypes.bfloat16


def bf(x):
    return np.asarray(x, np.float32).astype(BF16)


def f32(x):
    return np.asarray(x, np.float32)


def f64(x):
    return np.asarray(x).astype(np.float64)


def striped(idx):
    return np.tile(idx.reshape(-1, 16).T, (8, 1))


D, V, T, B, N = 128, 2048, 1024, 4, 4096
BETA1 = 2.0
NEG = -1e30


def setup_inputs():
    return {
        "table": bf(np.random.standard_normal((D, V))),
        "wv": bf(np.random.standard_normal((D, D)) / np.sqrt(D)),
        "pos": bf(np.random.standard_normal((T, T))),
        "wq": bf(np.random.standard_normal((T, T)) / np.sqrt(T)),
        "wk": bf(np.random.standard_normal((T, T)) / np.sqrt(T)),
        "offs": striped(np.random.permutation(np.tile(np.arange(V), 2))[:N]),
    }


def reference(table, wv, pos, wq, wk, offs):
    idx = offs[:16].T.reshape(-1)
    q = f64(wq).T @ f64(pos)
    k = f64(wk).T @ f64(pos)
    sc = BETA1 * (q.T @ k) / np.sqrt(T)
    keep = np.arange(T)[None, :] <= np.arange(T)[:, None]
    sc = np.where(keep, sc, NEG)
    ex = np.exp(sc - sc.max(axis=1, keepdims=True))
    a = ex / ex.sum(axis=1, keepdims=True)
    a[0, :] = 0.0
    e = f64(table)[:, idx]
    v = f64(wv).T @ e
    y = (v.reshape(D * B, T) @ a.T).reshape(D, N)
    return np.concatenate([e + y, e], axis=0)

@@ -1,0 +1,165 @@
+import concourse.mybir as mybir
+from concourse.masks import make_identity
+
+P = 128
+D, V, T, B = 128, 2048, 1024, 4
+N = B * T
+BANK = 512
+NB = T // P
+HALVES = T // BANK
+NEG = -1e30
+
+FLOPS = 2 * (2 * T * T * T + T * (T * (T + 1) // 2) + D * D * N + D * B * (T * (T + 1) // 2))
+
+BF16, F32, U16, I32 = mybir.dt.bfloat16, mybir.dt.float32, mybir.dt.uint16, mybir.dt.int32
+ACT = mybir.ActivationFunctionType
+ALU = mybir.AluOpType
+X = mybir.AxisListType.X
+
+
+def tile_lin_sfm_attention_b_kernel(tc, table, wv, pos, wq, wk, offs, out):
+    nc = tc.nc
+    with (
+        tc.tile_pool(name="held", bufs=1) as held,
+        tc.tile_pool(name="work", bufs=2) as work,
+        tc.tile_pool(name="small", bufs=4) as small,
+        tc.tile_pool(name="store", bufs=3) as store,
+        tc.psum_pool(name="banks", bufs=6) as banks,
+        tc.psum_pool(name="flipped", bufs=2) as flipped,
+    ):
+        offsets = held.tile([P, N // 16], U16, name="offsets")
+        nc.sync.dma_start(offsets[:], offs)
+        table_sb = held.tile([P, V], BF16, name="table_sb")
+        nc.sync.dma_start(table_sb[:], table)
+        wv_sb = held.tile([P, D], BF16, name="wv_sb")
+        nc.scalar.dma_start(wv_sb[:], wv)
+        pos_sb = held.tile([P, NB, T], BF16, name="pos_sb")
+        wk_sb = held.tile([P, NB, T], BF16, name="wk_sb")
+        wq_sb = held.tile([P, NB, T], BF16, name="wq_sb")
+        for dst, src in ((pos_sb, pos), (wk_sb, wk), (wq_sb, wq)):
+            blocks = src.rearrange("(r p) c -> p r c", p=P)
+            nc.sync.dma_start(dst[:, 0 : NB // 2, :], blocks[:, 0 : NB // 2, :])
+            nc.scalar.dma_start(dst[:, NB // 2 : NB, :], blocks[:, NB // 2 : NB, :])
+
+        ident = held.tile([P, P], BF16, name="ident")
+        make_identity(nc, ident[:])
+        ahead = held.tile([P, P], I32, name="ahead")
+        nc.gpsimd.iota(ahead[:], pattern=[[1, P]], base=0, channel_multiplier=-1)
+        mask = held.tile([P, P], BF16, name="mask")
+        nc.vector.tensor_scalar(mask[:], ahead[:], 0.0, NEG, op0=ALU.is_gt, op1=ALU.mult)
+
+        v_sb = held.tile([P, N], BF16, name="v_sb")
+        e_sb = held.tile([P, N], F32, name="e_sb")
+        for c in range(N // BANK):
+            cols = slice(c * BANK, (c + 1) * BANK)
+            piece = offsets[:, c * (BANK // 16) : (c + 1) * (BANK // 16)]
+            v_ps = banks.tile([P, BANK], F32, name="v_ps", tag="bank")
+            nc.tensor.matmul(v_ps[:], wv_sb[:], table_sb[:].indirect(piece), start=True, stop=True)
+            nc.vector.tensor_copy(v_sb[:, cols], v_ps[:])
+            e_ps = banks.tile([P, BANK], F32, name="e_ps", tag="bank")
+            nc.tensor.matmul(e_ps[:], ident[:], table_sb[:].indirect(piece), start=True, stop=True)
+            nc.scalar.activation(e_sb[:, cols], e_ps[:], ACT.Copy)
+            nc.sync.dma_start(out[D : 2 * D, cols], e_sb[:, cols])
+
+        vT_sb = held.tile([P, N], BF16, name="vT_sb")
+        for g in range(N // T):
+            vT_ps = flipped.tile([P, T], BF16, name="vT_ps", tag="flip")
+            for j in range(NB):
+                cols = slice(j * P, (j + 1) * P)
+                nc.tensor.transpose(vT_ps[:, cols], v_sb[:, g * T + j * P : g * T + (j + 1) * P], ident[:])
+            nc.vector.tensor_copy(vT_sb[:, g * T : (g + 1) * T], vT_ps[:])
+
+        k_sb = held.tile([P, NB, T], BF16, name="k_sb")
+        q_sb = held.tile([P, NB, T], BF16, name="q_sb")
+
+        def project(dst, w_sb, scale, h):
+            cols = slice(h * BANK, (h + 1) * BANK)
+            for ub in range(NB):
+                acc = banks.tile([P, BANK], F32, name="acc", tag="bank")
+                for r in range(NB):
+                    nc.tensor.matmul(
+                        acc[:], w_sb[:, r, ub * P : (ub + 1) * P], pos_sb[:, r, cols], start=(r == 0), stop=(r == NB - 1)
+                    )
+                if ub % 2 == 0:
+                    nc.vector.tensor_scalar_mul(dst[:, ub, cols], acc[:], scale)
+                else:
+                    nc.scalar.activation(dst[:, ub, cols], acc[:], ACT.Copy, scale=scale)
+
+        aT_sb = held.tile([P, NB, T], BF16, name="aT_sb")
+
+        def attend(i):
+            width = (i + 1) * P
+            chunks = [(lo, min(BANK, width - lo)) for lo in range(0, width, BANK)]
+            n = len(chunks)
+            rows = slice(i * P, (i + 1) * P)
+            peak = small.tile([P, HALVES], F32, name="peak", tag="peak")
+            part = small.tile([P, HALVES], F32, name="part", tag="part")
+            sc_ps = []
+            for c, (lo, w) in enumerate(chunks):
+                sc = banks.tile([P, BANK], F32, name="sc", tag="bank")
+                sc_ps.append(sc)
+                diagonal = c == n - 1
+                for ub in range(NB):
+                    nc.tensor.matmul(
+                        sc[:, 0:w],
+                        q_sb[:, ub, rows],
+                        k_sb[:, ub, lo : lo + w],
+                        start=(ub == 0),
+                        stop=(ub == NB - 1 and not diagonal),
+                    )
+                if diagonal:
+                    nc.tensor.matmul(sc[:, w - P : w], ident[:], mask[:], start=False, stop=True)
+                nc.vector.reduce_max(peak[:, c : c + 1], sc[:, 0:w], axis=X)
+            negmax = small.tile([P, 1], F32, name="negmax", tag="negmax")
+            nc.vector.reduce_max(negmax[:], peak[:, 0:n], axis=X, negate=True)
+            ex = work.tile([P, T], F32, name="ex", tag="ex")
+            for c, (lo, w) in enumerate(chunks):
+                nc.scalar.activation(
+                    ex[:, lo : lo + w], sc_ps[c][:, 0:w], ACT.Exp, bias=negmax[:], scale=1.0, accum_out=part[:, c : c + 1]
+                )
+            total = small.tile([P, 1], F32, name="total", tag="total")
+            nc.vector.reduce_sum(total[:], part[:, 0:n], axis=X)
+            rsum = small.tile([P, 1], F32, name="rsum", tag="rsum")
+            nc.vector.reciprocal(rsum[:], total[:])
+            if i == 0:
+                nc.vector.memset(rsum[0:1, :], 0.0)
+            a = work.tile([P, T], BF16, name="a", tag="a")
+            nc.vector.tensor_scalar_mul(a[:, 0:width], ex[:, 0:width], rsum[:])
+            aT_ps = flipped.tile([P, T], BF16, name="aT_ps", tag="flip")
+            for tb in range(i + 1):
+                cols = slice(tb * P, (tb + 1) * P)
+                nc.tensor.transpose(aT_ps[:, cols], a[:, cols], ident[:])
+            nc.scalar.activation(
+                aT_sb[:, 0 : i + 1, rows], aT_ps[:, 0:width].rearrange("p (tb s) -> p tb s", s=P), ACT.Copy
+            )
+
+        def mix(h):
+            first, end = h * BANK, (h + 1) * BANK
+            last_tb = end // P - 1
+            for b in range(B):
+                y_ps = banks.tile([P, BANK], F32, name="y_ps", tag="bank")
+                for tb in range(last_tb + 1):
+                    lo = max(tb * P, first)
+                    nc.tensor.matmul(
+                        y_ps[:, lo - first : BANK],
+                        vT_sb[:, (b * NB + tb) * P : (b * NB + tb + 1) * P],
+                        aT_sb[:, tb, lo:end],
+                        start=(tb == 0),
+                        stop=(tb == last_tb),
+                    )
+                cols = slice(b * T + first, b * T + end)
+                res = store.tile([P, BANK], F32, name="res", tag="res")
+                nc.vector.tensor_tensor(res[:], y_ps[:], e_sb[:, cols], ALU.add)
+                nc.sync.dma_start(out[0:D, cols], res[:])
+
+        q_scale = 2.0 / (T**0.5)
+        project(k_sb, wk_sb, 1.0, 0)
+        project(k_sb, wk_sb, 1.0, 1)
+        project(q_sb, wq_sb, q_scale, 1)
+        for i in (7, 6, 5, 4):
+            attend(i)
+        project(q_sb, wq_sb, q_scale, 0)
+        for i in (3, 2, 1, 0):
+            attend(i)
+        mix(1)
+        mix(0)

@@ -9,7 +9,7 @@ NB = T // P
 HALVES = T // BANK
 NEG = -1e30
 
-FLOPS = 2 * (2 * T * T * T + T * (T * (T + 1) // 2) + D * D * N + D * B * (T * (T + 1) // 2))
+FLOPS = 2 * (2 * T * T * T + T * (T * (T + 1) // 2) + D * B * (T * (T + 1) // 2) + D * D * N)
 
 BF16, F32, U16, I32 = mybir.dt.bfloat16, mybir.dt.float32, mybir.dt.uint16, mybir.dt.int32
 ACT = mybir.ActivationFunctionType
@@ -22,8 +22,7 @@ def tile_lin_sfm_attention_b_kernel(tc, table, wv, pos, wq, wk, offs, out):
     with (
         tc.tile_pool(name="held", bufs=1) as held,
         tc.tile_pool(name="work", bufs=2) as work,
-        tc.tile_pool(name="small", bufs=4) as small,
-        tc.tile_pool(name="store", bufs=3) as store,
+        tc.tile_pool(name="small", bufs=2) as small,
         tc.psum_pool(name="banks", bufs=6) as banks,
         tc.psum_pool(name="flipped", bufs=2) as flipped,
     ):
@@ -51,47 +50,46 @@ def tile_lin_sfm_attention_b_kernel(tc, table, wv, pos, wq, wk, offs, out):
         v_sb = held.tile([P, N], BF16, name="v_sb")
         e_sb = held.tile([P, N], F32, name="e_sb")
         for c in range(N // BANK):
-            cols = slice(c * BANK, (c + 1) * BANK)
+            entries = slice(c * BANK, (c + 1) * BANK)
             piece = offsets[:, c * (BANK // 16) : (c + 1) * (BANK // 16)]
             v_ps = banks.tile([P, BANK], F32, name="v_ps", tag="bank")
             nc.tensor.matmul(v_ps[:], wv_sb[:], table_sb[:].indirect(piece), start=True, stop=True)
-            nc.vector.tensor_copy(v_sb[:, cols], v_ps[:])
+            nc.vector.tensor_copy(v_sb[:, entries], v_ps[:])
             e_ps = banks.tile([P, BANK], F32, name="e_ps", tag="bank")
             nc.tensor.matmul(e_ps[:], ident[:], table_sb[:].indirect(piece), start=True, stop=True)
-            nc.scalar.activation(e_sb[:, cols], e_ps[:], ACT.Copy)
-            nc.sync.dma_start(out[D : 2 * D, cols], e_sb[:, cols])
+            nc.scalar.activation(e_sb[:, entries], e_ps[:], ACT.Copy)
+            nc.sync.dma_start(out[D : 2 * D, entries], e_sb[:, entries])
 
         vT_sb = held.tile([P, N], BF16, name="vT_sb")
-        for g in range(N // T):
+        for b in range(B):
             vT_ps = flipped.tile([P, T], BF16, name="vT_ps", tag="flip")
-            for j in range(NB):
-                cols = slice(j * P, (j + 1) * P)
-                nc.tensor.transpose(vT_ps[:, cols], v_sb[:, g * T + j * P : g * T + (j + 1) * P], ident[:])
-            nc.vector.tensor_copy(vT_sb[:, g * T : (g + 1) * T], vT_ps[:])
+            for tb in range(NB):
+                nc.tensor.transpose(
+                    vT_ps[:, tb * P : (tb + 1) * P], v_sb[:, b * T + tb * P : b * T + (tb + 1) * P], ident[:]
+                )
+            nc.vector.tensor_copy(vT_sb[:, b * T : (b + 1) * T], vT_ps[:])
 
         k_sb = held.tile([P, NB, T], BF16, name="k_sb")
         q_sb = held.tile([P, NB, T], BF16, name="q_sb")
 
         def project(dst, w_sb, scale, h):
-            cols = slice(h * BANK, (h + 1) * BANK)
+            half = slice(h * BANK, (h + 1) * BANK)
             for ub in range(NB):
                 acc = banks.tile([P, BANK], F32, name="acc", tag="bank")
                 for r in range(NB):
                     nc.tensor.matmul(
-                        acc[:], w_sb[:, r, ub * P : (ub + 1) * P], pos_sb[:, r, cols], start=(r == 0), stop=(r == NB - 1)
+                        acc[:], w_sb[:, r, ub * P : (ub + 1) * P], pos_sb[:, r, half], start=(r == 0), stop=(r == NB - 1)
                     )
                 if ub % 2 == 0:
-                    nc.vector.tensor_scalar_mul(dst[:, ub, cols], acc[:], scale)
+                    nc.vector.tensor_scalar_mul(dst[:, ub, half], acc[:], scale)
                 else:
-                    nc.scalar.activation(dst[:, ub, cols], acc[:], ACT.Copy, scale=scale)
+                    nc.scalar.activation(dst[:, ub, half], acc[:], ACT.Copy, scale=scale)
 
-        aT_sb = held.tile([P, NB, T], BF16, name="aT_sb")
-
-        def attend(i):
+        def weights(i):
+            queries = slice(i * P, (i + 1) * P)
             width = (i + 1) * P
             chunks = [(lo, min(BANK, width - lo)) for lo in range(0, width, BANK)]
             n = len(chunks)
-            rows = slice(i * P, (i + 1) * P)
             peak = small.tile([P, HALVES], F32, name="peak", tag="peak")
             part = small.tile([P, HALVES], F32, name="part", tag="part")
             sc_ps = []
@@ -102,7 +100,7 @@ def tile_lin_sfm_attention_b_kernel(tc, table, wv, pos, wq, wk, offs, out):
                 for ub in range(NB):
                     nc.tensor.matmul(
                         sc[:, 0:w],
-                        q_sb[:, ub, rows],
+                        q_sb[:, ub, queries],
                         k_sb[:, ub, lo : lo + w],
                         start=(ub == 0),
                         stop=(ub == NB - 1 and not diagonal),
@@ -125,41 +123,59 @@ def tile_lin_sfm_attention_b_kernel(tc, table, wv, pos, wq, wk, offs, out):
                 nc.vector.memset(rsum[0:1, :], 0.0)
             a = work.tile([P, T], BF16, name="a", tag="a")
             nc.vector.tensor_scalar_mul(a[:, 0:width], ex[:, 0:width], rsum[:])
+            return a
+
+        aT_sb = held.tile([P, NB, T], BF16, name="aT_sb")
+
+        def flip(i, a):
+            queries = slice(i * P, (i + 1) * P)
             aT_ps = flipped.tile([P, T], BF16, name="aT_ps", tag="flip")
             for tb in range(i + 1):
-                cols = slice(tb * P, (tb + 1) * P)
-                nc.tensor.transpose(aT_ps[:, cols], a[:, cols], ident[:])
+                nc.tensor.transpose(aT_ps[:, tb * P : (tb + 1) * P], a[:, tb * P : (tb + 1) * P], ident[:])
             nc.scalar.activation(
-                aT_sb[:, 0 : i + 1, rows], aT_ps[:, 0:width].rearrange("p (tb s) -> p tb s", s=P), ACT.Copy
+                aT_sb[:, 0 : i + 1, queries], aT_ps[:, 0 : (i + 1) * P].rearrange("p (tb s) -> p tb s", s=P), ACT.Copy
             )
 
-        def mix(h):
+        res_sb = held.tile([P, N], F32, name="res_sb")
+
+        def mix(h, b):
             first, end = h * BANK, (h + 1) * BANK
             last_tb = end // P - 1
-            for b in range(B):
-                y_ps = banks.tile([P, BANK], F32, name="y_ps", tag="bank")
-                for tb in range(last_tb + 1):
-                    lo = max(tb * P, first)
-                    nc.tensor.matmul(
-                        y_ps[:, lo - first : BANK],
-                        vT_sb[:, (b * NB + tb) * P : (b * NB + tb + 1) * P],
-                        aT_sb[:, tb, lo:end],
-                        start=(tb == 0),
-                        stop=(tb == last_tb),
-                    )
-                cols = slice(b * T + first, b * T + end)
-                res = store.tile([P, BANK], F32, name="res", tag="res")
-                nc.vector.tensor_tensor(res[:], y_ps[:], e_sb[:, cols], ALU.add)
-                nc.sync.dma_start(out[0:D, cols], res[:])
+            y_ps = banks.tile([P, BANK], F32, name="y_ps", tag="bank")
+            for tb in range(last_tb + 1):
+                lo = max(tb * P, first)
+                nc.tensor.matmul(
+                    y_ps[:, lo - first : BANK],
+                    vT_sb[:, (b * NB + tb) * P : (b * NB + tb + 1) * P],
+                    aT_sb[:, tb, lo:end],
+                    start=(tb == 0),
+                    stop=(tb == last_tb),
+                )
+            entries = slice(b * T + first, b * T + end)
+            nc.vector.tensor_tensor(res_sb[:, entries], y_ps[:], e_sb[:, entries], ALU.add)
+            nc.sync.dma_start(out[0:D, entries], res_sb[:, entries])
 
-        q_scale = 2.0 / (T**0.5)
+        q_scale = 2.0 / T**0.5
         project(k_sb, wk_sb, 1.0, 0)
         project(k_sb, wk_sb, 1.0, 1)
         project(q_sb, wq_sb, q_scale, 1)
-        for i in (7, 6, 5, 4):
-            attend(i)
+        unflipped = None
+        for i in range(NB - 1, NB // 2 - 1, -1):
+            a = weights(i)
+            if unflipped is not None:
+                flip(*unflipped)
+            unflipped = (i, a)
         project(q_sb, wq_sb, q_scale, 0)
-        for i in (3, 2, 1, 0):
-            attend(i)
-        mix(1)
-        mix(0)
+        for i in range(NB // 2 - 1, 0, -1):
+            a = weights(i)
+            flip(*unflipped)
+            unflipped = (i, a)
+        a = weights(0)
+        mix(1, 0)
+        mix(1, 1)
+        flip(*unflipped)
+        flip(0, a)
+        mix(1, 2)
+        mix(1, 3)
+        for b in range(B):
+            mix(0, b)

@@ -35,10 +35,16 @@ def tile_lin_sfm_attention_b_kernel(tc, table, wv, pos, wq, wk, offs, out):
         pos_sb = held.tile([P, NB, T], BF16, name="pos_sb")
         wk_sb = held.tile([P, NB, T], BF16, name="wk_sb")
         wq_sb = held.tile([P, NB, T], BF16, name="wq_sb")
-        for dst, src in ((pos_sb, pos), (wk_sb, wk), (wq_sb, wq)):
+
+        def load(dst, src, columns):
             blocks = src.rearrange("(r p) c -> p r c", p=P)
-            nc.sync.dma_start(dst[:, 0 : NB // 2, :], blocks[:, 0 : NB // 2, :])
-            nc.scalar.dma_start(dst[:, NB // 2 : NB, :], blocks[:, NB // 2 : NB, :])
+            nc.sync.dma_start(dst[:, 0 : NB // 2, columns], blocks[:, 0 : NB // 2, columns])
+            nc.scalar.dma_start(dst[:, NB // 2 : NB, columns], blocks[:, NB // 2 : NB, columns])
+
+        load(pos_sb, pos, slice(0, BANK))
+        load(wk_sb, wk, slice(0, T))
+        load(pos_sb, pos, slice(BANK, T))
+        load(wq_sb, wq, slice(0, T))
 
         ident = held.tile([P, P], BF16, name="ident")
         make_identity(nc, ident[:])
@@ -49,9 +55,9 @@ def tile_lin_sfm_attention_b_kernel(tc, table, wv, pos, wq, wk, offs, out):
 
         v_sb = held.tile([P, N], BF16, name="v_sb")
         e_sb = held.tile([P, N], F32, name="e_sb")
-        for c in range(N // BANK):
-            entries = slice(c * BANK, (c + 1) * BANK)
-            piece = offsets[:, c * (BANK // 16) : (c + 1) * (BANK // 16)]
+        for j in range(0, N, BANK):
+            entries = slice(j, j + BANK)
+            piece = offsets[:, j // 16 : (j + BANK) // 16]
             v_ps = banks.tile([P, BANK], F32, name="v_ps", tag="bank")
             nc.tensor.matmul(v_ps[:], wv_sb[:], table_sb[:].indirect(piece), start=True, stop=True)
             nc.vector.tensor_copy(v_sb[:, entries], v_ps[:])
@@ -61,7 +67,8 @@ def tile_lin_sfm_attention_b_kernel(tc, table, wv, pos, wq, wk, offs, out):
             nc.sync.dma_start(out[D : 2 * D, entries], e_sb[:, entries])
 
         vT_sb = held.tile([P, N], BF16, name="vT_sb")
-        for b in range(B):
+
+        def flip_v(b):
             vT_ps = flipped.tile([P, T], BF16, name="vT_ps", tag="flip")
             for tb in range(NB):
                 nc.tensor.transpose(
@@ -88,32 +95,32 @@ def tile_lin_sfm_attention_b_kernel(tc, table, wv, pos, wq, wk, offs, out):
         def weights(i):
             queries = slice(i * P, (i + 1) * P)
             width = (i + 1) * P
-            chunks = [(lo, min(BANK, width - lo)) for lo in range(0, width, BANK)]
+            chunks = [(lo, min(lo + BANK, width)) for lo in range(0, width, BANK)]
             n = len(chunks)
             peak = small.tile([P, HALVES], F32, name="peak", tag="peak")
             part = small.tile([P, HALVES], F32, name="part", tag="part")
             sc_ps = []
-            for c, (lo, w) in enumerate(chunks):
+            for c, (lo, hi) in enumerate(chunks):
                 sc = banks.tile([P, BANK], F32, name="sc", tag="bank")
                 sc_ps.append(sc)
                 diagonal = c == n - 1
                 for ub in range(NB):
                     nc.tensor.matmul(
-                        sc[:, 0:w],
+                        sc[:, 0 : hi - lo],
                         q_sb[:, ub, queries],
-                        k_sb[:, ub, lo : lo + w],
+                        k_sb[:, ub, lo:hi],
                         start=(ub == 0),
                         stop=(ub == NB - 1 and not diagonal),
                     )
                 if diagonal:
-                    nc.tensor.matmul(sc[:, w - P : w], ident[:], mask[:], start=False, stop=True)
-                nc.vector.reduce_max(peak[:, c : c + 1], sc[:, 0:w], axis=X)
+                    nc.tensor.matmul(sc[:, hi - lo - P : hi - lo], ident[:], mask[:], start=False, stop=True)
+                nc.vector.reduce_max(peak[:, c : c + 1], sc[:, 0 : hi - lo], axis=X)
             negmax = small.tile([P, 1], F32, name="negmax", tag="negmax")
             nc.vector.reduce_max(negmax[:], peak[:, 0:n], axis=X, negate=True)
             ex = work.tile([P, T], F32, name="ex", tag="ex")
-            for c, (lo, w) in enumerate(chunks):
+            for c, (lo, hi) in enumerate(chunks):
                 nc.scalar.activation(
-                    ex[:, lo : lo + w], sc_ps[c][:, 0:w], ACT.Exp, bias=negmax[:], scale=1.0, accum_out=part[:, c : c + 1]
+                    ex[:, lo:hi], sc_ps[c][:, 0 : hi - lo], ACT.Exp, bias=negmax[:], scale=1.0, accum_out=part[:, c : c + 1]
                 )
             total = small.tile([P, 1], F32, name="total", tag="total")
             nc.vector.reduce_sum(total[:], part[:, 0:n], axis=X)
@@ -139,26 +146,29 @@ def tile_lin_sfm_attention_b_kernel(tc, table, wv, pos, wq, wk, offs, out):
         res_sb = held.tile([P, N], F32, name="res_sb")
 
         def mix(h, b):
-            first, end = h * BANK, (h + 1) * BANK
-            last_tb = end // P - 1
+            s_first, s_end = h * BANK, (h + 1) * BANK
+            last_tb = s_end // P - 1
             y_ps = banks.tile([P, BANK], F32, name="y_ps", tag="bank")
             for tb in range(last_tb + 1):
-                lo = max(tb * P, first)
+                s_from = max(tb * P, s_first)
                 nc.tensor.matmul(
-                    y_ps[:, lo - first : BANK],
+                    y_ps[:, s_from - s_first : BANK],
                     vT_sb[:, (b * NB + tb) * P : (b * NB + tb + 1) * P],
-                    aT_sb[:, tb, lo:end],
+                    aT_sb[:, tb, s_from:s_end],
                     start=(tb == 0),
                     stop=(tb == last_tb),
                 )
-            entries = slice(b * T + first, b * T + end)
+            entries = slice(b * T + s_first, b * T + s_end)
             nc.vector.tensor_tensor(res_sb[:, entries], y_ps[:], e_sb[:, entries], ALU.add)
             nc.sync.dma_start(out[0:D, entries], res_sb[:, entries])
 
         q_scale = 2.0 / T**0.5
         project(k_sb, wk_sb, 1.0, 0)
+        flip_v(0)
         project(k_sb, wk_sb, 1.0, 1)
+        flip_v(1)
         project(q_sb, wq_sb, q_scale, 1)
+        flip_v(2)
         unflipped = None
         for i in range(NB - 1, NB // 2 - 1, -1):
             a = weights(i)
@@ -166,6 +176,7 @@ def tile_lin_sfm_attention_b_kernel(tc, table, wv, pos, wq, wk, offs, out):
                 flip(*unflipped)
             unflipped = (i, a)
         project(q_sb, wq_sb, q_scale, 0)
+        flip_v(3)
         for i in range(NB // 2 - 1, 0, -1):
             a = weights(i)
             flip(*unflipped)

@@ -163,12 +163,11 @@ def tile_lin_sfm_attention_b_kernel(tc, table, wv, pos, wq, wk, offs, out):
             nc.sync.dma_start(out[0:D, entries], res_sb[:, entries])
 
         q_scale = 2.0 / T**0.5
+        for b in range(B):
+            flip_v(b)
         project(k_sb, wk_sb, 1.0, 0)
-        flip_v(0)
         project(k_sb, wk_sb, 1.0, 1)
-        flip_v(1)
         project(q_sb, wq_sb, q_scale, 1)
-        flip_v(2)
         unflipped = None
         for i in range(NB - 1, NB // 2 - 1, -1):
             a = weights(i)
@@ -176,7 +175,6 @@ def tile_lin_sfm_attention_b_kernel(tc, table, wv, pos, wq, wk, offs, out):
                 flip(*unflipped)
             unflipped = (i, a)
         project(q_sb, wq_sb, q_scale, 0)
-        flip_v(3)
         for i in range(NB // 2 - 1, 0, -1):
             a = weights(i)
             flip(*unflipped)

@@ -8,6 +8,7 @@ BANK = 512
 NB = T // P
 HALVES = T // BANK
 NEG = -1e30
+WARM = 6
 
 FLOPS = 2 * (2 * T * T * T + T * (T * (T + 1) // 2) + D * B * (T * (T + 1) // 2) + D * D * N)
 
@@ -52,6 +53,12 @@ def tile_lin_sfm_attention_b_kernel(tc, table, wv, pos, wq, wk, offs, out):
         nc.gpsimd.iota(ahead[:], pattern=[[1, P]], base=0, channel_multiplier=-1)
         mask = held.tile([P, P], BF16, name="mask")
         nc.vector.tensor_scalar(mask[:], ahead[:], 0.0, NEG, op0=ALU.is_gt, op1=ALU.mult)
+
+        zeros = held.tile([P, BANK], BF16, name="zeros")
+        nc.vector.memset(zeros[:], 0.0)
+        warm_ps = banks.tile([P, BANK], F32, name="warm_ps", tag="bank")
+        for n in range(WARM):
+            nc.tensor.matmul(warm_ps[:], zeros[:, 0:P], zeros[:], start=True, stop=True)
 
         v_sb = held.tile([P, N], BF16, name="v_sb")
         e_sb = held.tile([P, N], F32, name="e_sb")
@@ -163,11 +170,12 @@ def tile_lin_sfm_attention_b_kernel(tc, table, wv, pos, wq, wk, offs, out):
             nc.sync.dma_start(out[0:D, entries], res_sb[:, entries])
 
         q_scale = 2.0 / T**0.5
-        for b in range(B):
-            flip_v(b)
         project(k_sb, wk_sb, 1.0, 0)
+        flip_v(0)
         project(k_sb, wk_sb, 1.0, 1)
+        flip_v(1)
         project(q_sb, wq_sb, q_scale, 1)
+        flip_v(2)
         unflipped = None
         for i in range(NB - 1, NB // 2 - 1, -1):
             a = weights(i)
@@ -175,6 +183,7 @@ def tile_lin_sfm_attention_b_kernel(tc, table, wv, pos, wq, wk, offs, out):
                 flip(*unflipped)
             unflipped = (i, a)
         project(q_sb, wq_sb, q_scale, 0)
+        flip_v(3)
         for i in range(NB // 2 - 1, 0, -1):
             a = weights(i)
             flip(*unflipped)

@@ -23,6 +23,7 @@ def tile_lin_sfm_attention_b_kernel(tc, table, wv, pos, wq, wk, offs, out):
     with (
         tc.tile_pool(name="held", bufs=1) as held,
         tc.tile_pool(name="work", bufs=2) as work,
+        tc.tile_pool(name="unflipped", bufs=4) as unflipped,
         tc.tile_pool(name="small", bufs=2) as small,
         tc.psum_pool(name="banks", bufs=6) as banks,
         tc.psum_pool(name="flipped", bufs=2) as flipped,
@@ -75,19 +76,17 @@ def tile_lin_sfm_attention_b_kernel(tc, table, wv, pos, wq, wk, offs, out):
 
         vT_sb = held.tile([P, N], BF16, name="vT_sb")
 
-        def flip_v(b):
-            vT_ps = flipped.tile([P, T], BF16, name="vT_ps", tag="flip")
-            for tb in range(NB):
-                nc.tensor.transpose(
-                    vT_ps[:, tb * P : (tb + 1) * P], v_sb[:, b * T + tb * P : b * T + (tb + 1) * P], ident[:]
-                )
-            nc.vector.tensor_copy(vT_sb[:, b * T : (b + 1) * T], vT_ps[:])
+        def flip_block(bank, guest, n):
+            src, blocks = guest
+            if n < blocks:
+                nc.tensor.transpose(bank[:, n * P : (n + 1) * P], src[:, n * P : (n + 1) * P], ident[:])
 
         k_sb = held.tile([P, NB, T], BF16, name="k_sb")
         q_sb = held.tile([P, NB, T], BF16, name="q_sb")
 
-        def project(dst, w_sb, scale, h):
+        def project(dst, w_sb, scale, h, b):
             half = slice(h * BANK, (h + 1) * BANK)
+            vT_ps = flipped.tile([P, T], BF16, name="vT_ps", tag="flip")
             for ub in range(NB):
                 acc = banks.tile([P, BANK], F32, name="acc", tag="bank")
                 for r in range(NB):
@@ -98,8 +97,19 @@ def tile_lin_sfm_attention_b_kernel(tc, table, wv, pos, wq, wk, offs, out):
                     nc.vector.tensor_scalar_mul(dst[:, ub, half], acc[:], scale)
                 else:
                     nc.scalar.activation(dst[:, ub, half], acc[:], ACT.Copy, scale=scale)
+                flip_block(vT_ps, (v_sb[:, b * T : (b + 1) * T], NB), ub)
+            nc.vector.tensor_copy(vT_sb[:, b * T : (b + 1) * T], vT_ps[:])
 
-        def weights(i):
+        aT_sb = held.tile([P, NB, T], BF16, name="aT_sb")
+
+        def keep_flipped(g, aT_ps):
+            nc.scalar.activation(
+                aT_sb[:, 0 : g + 1, g * P : (g + 1) * P],
+                aT_ps[:, 0 : (g + 1) * P].rearrange("p (tb s) -> p tb s", s=P),
+                ACT.Copy,
+            )
+
+        def weights(i, g=None, a_g=None):
             queries = slice(i * P, (i + 1) * P)
             width = (i + 1) * P
             chunks = [(lo, min(lo + BANK, width)) for lo in range(0, width, BANK)]
@@ -107,6 +117,8 @@ def tile_lin_sfm_attention_b_kernel(tc, table, wv, pos, wq, wk, offs, out):
             peak = small.tile([P, HALVES], F32, name="peak", tag="peak")
             part = small.tile([P, HALVES], F32, name="part", tag="part")
             sc_ps = []
+            if g is not None:
+                aT_ps = flipped.tile([P, T], BF16, name="aT_ps", tag="flip")
             for c, (lo, hi) in enumerate(chunks):
                 sc = banks.tile([P, BANK], F32, name="sc", tag="bank")
                 sc_ps.append(sc)
@@ -119,6 +131,10 @@ def tile_lin_sfm_attention_b_kernel(tc, table, wv, pos, wq, wk, offs, out):
                         start=(ub == 0),
                         stop=(ub == NB - 1 and not diagonal),
                     )
+                    if g is not None and c == 0:
+                        flip_block(aT_ps, (a_g, g + 1), ub)
+                if g is not None and c == 0:
+                    keep_flipped(g, aT_ps)
                 if diagonal:
                     nc.tensor.matmul(sc[:, hi - lo - P : hi - lo], ident[:], mask[:], start=False, stop=True)
                 nc.vector.reduce_max(peak[:, c : c + 1], sc[:, 0 : hi - lo], axis=X)
@@ -135,27 +151,18 @@ def tile_lin_sfm_attention_b_kernel(tc, table, wv, pos, wq, wk, offs, out):
             nc.vector.reciprocal(rsum[:], total[:])
             if i == 0:
                 nc.vector.memset(rsum[0:1, :], 0.0)
-            a = work.tile([P, T], BF16, name="a", tag="a")
+            a = unflipped.tile([P, T], BF16, name="a", tag="a")
             nc.vector.tensor_scalar_mul(a[:, 0:width], ex[:, 0:width], rsum[:])
             return a
 
-        aT_sb = held.tile([P, NB, T], BF16, name="aT_sb")
-
-        def flip(i, a):
-            queries = slice(i * P, (i + 1) * P)
-            aT_ps = flipped.tile([P, T], BF16, name="aT_ps", tag="flip")
-            for tb in range(i + 1):
-                nc.tensor.transpose(aT_ps[:, tb * P : (tb + 1) * P], a[:, tb * P : (tb + 1) * P], ident[:])
-            nc.scalar.activation(
-                aT_sb[:, 0 : i + 1, queries], aT_ps[:, 0 : (i + 1) * P].rearrange("p (tb s) -> p tb s", s=P), ACT.Copy
-            )
-
         res_sb = held.tile([P, N], F32, name="res_sb")
 
-        def mix(h, b):
+        def mix(h, b, g=None, a_g=None):
             s_first, s_end = h * BANK, (h + 1) * BANK
             last_tb = s_end // P - 1
             y_ps = banks.tile([P, BANK], F32, name="y_ps", tag="bank")
+            if g is not None:
+                aT_ps = flipped.tile([P, T], BF16, name="aT_ps", tag="flip")
             for tb in range(last_tb + 1):
                 s_from = max(tb * P, s_first)
                 nc.tensor.matmul(
@@ -165,35 +172,29 @@ def tile_lin_sfm_attention_b_kernel(tc, table, wv, pos, wq, wk, offs, out):
                     start=(tb == 0),
                     stop=(tb == last_tb),
                 )
+                if g is not None:
+                    flip_block(aT_ps, (a_g, g + 1), tb)
+            if g is not None:
+                keep_flipped(g, aT_ps)
             entries = slice(b * T + s_first, b * T + s_end)
             nc.vector.tensor_tensor(res_sb[:, entries], y_ps[:], e_sb[:, entries], ALU.add)
             nc.sync.dma_start(out[0:D, entries], res_sb[:, entries])
 
         q_scale = 2.0 / T**0.5
-        project(k_sb, wk_sb, 1.0, 0)
-        flip_v(0)
-        project(k_sb, wk_sb, 1.0, 1)
-        flip_v(1)
-        project(q_sb, wq_sb, q_scale, 1)
-        flip_v(2)
-        unflipped = None
-        for i in range(NB - 1, NB // 2 - 1, -1):
-            a = weights(i)
-            if unflipped is not None:
-                flip(*unflipped)
-            unflipped = (i, a)
-        project(q_sb, wq_sb, q_scale, 0)
-        flip_v(3)
-        for i in range(NB // 2 - 1, 0, -1):
-            a = weights(i)
-            flip(*unflipped)
-            unflipped = (i, a)
-        a = weights(0)
-        mix(1, 0)
-        mix(1, 1)
-        flip(*unflipped)
-        flip(0, a)
-        mix(1, 2)
-        mix(1, 3)
+        a = {}
+        project(k_sb, wk_sb, 1.0, 0, 0)
+        project(k_sb, wk_sb, 1.0, 1, 1)
+        project(q_sb, wq_sb, q_scale, 1, 2)
+        a[7] = weights(7)
+        a[6] = weights(6)
+        a[5] = weights(5, 7, a[7])
+        a[4] = weights(4, 6, a[6])
+        project(q_sb, wq_sb, q_scale, 0, 3)
+        a[3] = weights(3, 5, a[5])
+        a[2] = weights(2, 4, a[4])
+        a[1] = weights(1)
+        a[0] = weights(0)
+        for b in range(B):
+            mix(1, b, 3 - b, a[3 - b])
         for b in range(B):
             mix(0, b)

@@ -74,42 +74,48 @@ def tile_lin_sfm_attention_b_kernel(tc, table, wv, pos, wq, wk, offs, out):
             nc.scalar.activation(e_sb[:, entries], e_ps[:], ACT.Copy)
             nc.sync.dma_start(out[D : 2 * D, entries], e_sb[:, entries])
 
-        vT_sb = held.tile([P, N], BF16, name="vT_sb")
+        vT_sb = held.tile([P, B * NB, P], BF16, name="vT_sb")
+        aT_sb = held.tile([P, NB, T], BF16, name="aT_sb")
 
-        def flip_block(bank, guest, n):
-            src, blocks = guest
-            if n < blocks:
-                nc.tensor.transpose(bank[:, n * P : (n + 1) * P], src[:, n * P : (n + 1) * P], ident[:])
+        def flip_steps(guests):
+            return [(src, n, blocks, dst) for src, blocks, dst in guests for n in range(blocks)]
+
+        def flip_next(steps, bank):
+            if not steps:
+                return bank
+            src, n, blocks, dst = steps.pop(0)
+            if n == 0:
+                bank = flipped.tile([P, T], BF16, name="bank", tag="flip")
+            nc.tensor.transpose(bank[:, n * P : (n + 1) * P], src[:, n * P : (n + 1) * P], ident[:])
+            if n == blocks - 1:
+                nc.scalar.activation(dst, bank[:, 0 : blocks * P].rearrange("p (n c) -> p n c", c=P), ACT.Copy)
+            return bank
+
+        def v_guest(b):
+            return (v_sb[:, b * T : (b + 1) * T], NB, vT_sb[:, b * NB : (b + 1) * NB, :])
+
+        def a_guest(g, a_g):
+            return (a_g, g + 1, aT_sb[:, 0 : g + 1, g * P : (g + 1) * P])
 
         k_sb = held.tile([P, NB, T], BF16, name="k_sb")
         q_sb = held.tile([P, NB, T], BF16, name="q_sb")
 
-        def project(dst, w_sb, scale, h, b):
+        def project(dst, w_sb, scale, h, guests):
             half = slice(h * BANK, (h + 1) * BANK)
-            vT_ps = flipped.tile([P, T], BF16, name="vT_ps", tag="flip")
+            steps, bank = flip_steps(guests), None
             for ub in range(NB):
                 acc = banks.tile([P, BANK], F32, name="acc", tag="bank")
                 for r in range(NB):
                     nc.tensor.matmul(
                         acc[:], w_sb[:, r, ub * P : (ub + 1) * P], pos_sb[:, r, half], start=(r == 0), stop=(r == NB - 1)
                     )
+                    bank = flip_next(steps, bank)
                 if ub % 2 == 0:
                     nc.vector.tensor_scalar_mul(dst[:, ub, half], acc[:], scale)
                 else:
                     nc.scalar.activation(dst[:, ub, half], acc[:], ACT.Copy, scale=scale)
-                flip_block(vT_ps, (v_sb[:, b * T : (b + 1) * T], NB), ub)
-            nc.vector.tensor_copy(vT_sb[:, b * T : (b + 1) * T], vT_ps[:])
 
-        aT_sb = held.tile([P, NB, T], BF16, name="aT_sb")
-
-        def keep_flipped(g, aT_ps):
-            nc.scalar.activation(
-                aT_sb[:, 0 : g + 1, g * P : (g + 1) * P],
-                aT_ps[:, 0 : (g + 1) * P].rearrange("p (tb s) -> p tb s", s=P),
-                ACT.Copy,
-            )
-
-        def weights(i, g=None, a_g=None):
+        def weights(i, guests):
             queries = slice(i * P, (i + 1) * P)
             width = (i + 1) * P
             chunks = [(lo, min(lo + BANK, width)) for lo in range(0, width, BANK)]
@@ -117,8 +123,7 @@ def tile_lin_sfm_attention_b_kernel(tc, table, wv, pos, wq, wk, offs, out):
             peak = small.tile([P, HALVES], F32, name="peak", tag="peak")
             part = small.tile([P, HALVES], F32, name="part", tag="part")
             sc_ps = []
-            if g is not None:
-                aT_ps = flipped.tile([P, T], BF16, name="aT_ps", tag="flip")
+            steps, bank = flip_steps(guests), None
             for c, (lo, hi) in enumerate(chunks):
                 sc = banks.tile([P, BANK], F32, name="sc", tag="bank")
                 sc_ps.append(sc)
@@ -131,10 +136,7 @@ def tile_lin_sfm_attention_b_kernel(tc, table, wv, pos, wq, wk, offs, out):
                         start=(ub == 0),
                         stop=(ub == NB - 1 and not diagonal),
                     )
-                    if g is not None and c == 0:
-                        flip_block(aT_ps, (a_g, g + 1), ub)
-                if g is not None and c == 0:
-                    keep_flipped(g, aT_ps)
+                    bank = flip_next(steps, bank)
                 if diagonal:
                     nc.tensor.matmul(sc[:, hi - lo - P : hi - lo], ident[:], mask[:], start=False, stop=True)
                 nc.vector.reduce_max(peak[:, c : c + 1], sc[:, 0 : hi - lo], axis=X)
@@ -157,44 +159,46 @@ def tile_lin_sfm_attention_b_kernel(tc, table, wv, pos, wq, wk, offs, out):
 
         res_sb = held.tile([P, N], F32, name="res_sb")
 
-        def mix(h, b, g=None, a_g=None):
-            s_first, s_end = h * BANK, (h + 1) * BANK
+        def mix(s_first, s_end, b, guests):
+            width = s_end - s_first
             last_tb = s_end // P - 1
             y_ps = banks.tile([P, BANK], F32, name="y_ps", tag="bank")
-            if g is not None:
-                aT_ps = flipped.tile([P, T], BF16, name="aT_ps", tag="flip")
+            steps, bank = flip_steps(guests), None
             for tb in range(last_tb + 1):
                 s_from = max(tb * P, s_first)
                 nc.tensor.matmul(
-                    y_ps[:, s_from - s_first : BANK],
-                    vT_sb[:, (b * NB + tb) * P : (b * NB + tb + 1) * P],
+                    y_ps[:, s_from - s_first : width],
+                    vT_sb[:, b * NB + tb, :],
                     aT_sb[:, tb, s_from:s_end],
                     start=(tb == 0),
                     stop=(tb == last_tb),
                 )
-                if g is not None:
-                    flip_block(aT_ps, (a_g, g + 1), tb)
-            if g is not None:
-                keep_flipped(g, aT_ps)
+                bank = flip_next(steps, bank)
             entries = slice(b * T + s_first, b * T + s_end)
-            nc.vector.tensor_tensor(res_sb[:, entries], y_ps[:], e_sb[:, entries], ALU.add)
+            nc.vector.tensor_tensor(res_sb[:, entries], y_ps[:, 0:width], e_sb[:, entries], ALU.add)
             nc.sync.dma_start(out[0:D, entries], res_sb[:, entries])
 
         q_scale = 2.0 / T**0.5
-        a = {}
-        project(k_sb, wk_sb, 1.0, 0, 0)
-        project(k_sb, wk_sb, 1.0, 1, 1)
-        project(q_sb, wq_sb, q_scale, 1, 2)
-        a[7] = weights(7)
-        a[6] = weights(6)
-        a[5] = weights(5, 7, a[7])
-        a[4] = weights(4, 6, a[6])
-        project(q_sb, wq_sb, q_scale, 0, 3)
-        a[3] = weights(3, 5, a[5])
-        a[2] = weights(2, 4, a[4])
-        a[1] = weights(1)
-        a[0] = weights(0)
+        project(k_sb, wk_sb, 1.0, 0, [v_guest(0)])
+        project(k_sb, wk_sb, 1.0, 1, [v_guest(1)])
+        project(q_sb, wq_sb, q_scale, 1, [v_guest(2)])
+        a7 = weights(7, [])
+        a6 = weights(6, [])
+        a5 = weights(5, [])
+        a4 = weights(4, [a_guest(7, a7)])
+        project(q_sb, wq_sb, q_scale, 0, [v_guest(3), a_guest(6, a6), a_guest(5, a5), a_guest(4, a4)])
+        a3 = weights(3, [])
+        a2 = weights(2, [])
+        a1 = weights(1, [])
+        a0 = weights(0, [])
+        third, fourth = (2 * T // 4, 3 * T // 4), (3 * T // 4, T)
+        mix(*third, 0, [])
+        mix(*fourth, 0, [])
+        mix(*third, 1, [a_guest(3, a3)])
+        mix(*fourth, 1, [a_guest(2, a2)])
+        mix(*third, 2, [a_guest(1, a1)])
+        mix(*fourth, 2, [a_guest(0, a0)])
+        mix(*third, 3, [])
         for b in range(B):
-            mix(1, b, 3 - b, a[3 - b])
-        for b in range(B):
-            mix(0, b)
+            mix(0, BANK, b, [])
+        mix(*fourth, 3, [])

@@ -119,33 +119,31 @@ def tile_lin_sfm_attention_b_kernel(tc, table, wv, pos, wq, wk, offs, out):
             queries = slice(i * P, (i + 1) * P)
             width = (i + 1) * P
             chunks = [(lo, min(lo + BANK, width)) for lo in range(0, width, BANK)]
-            n = len(chunks)
-            peak = small.tile([P, HALVES], F32, name="peak", tag="peak")
-            part = small.tile([P, HALVES], F32, name="part", tag="part")
-            sc_ps = []
+            peak = small.tile([P, HALVES + 1], F32, name="peak", tag="peak")
+            part = small.tile([P, HALVES + 1], F32, name="part", tag="part")
+            pieces = []
             steps, bank = flip_steps(guests), None
-            for c, (lo, hi) in enumerate(chunks):
+            for lo, hi in chunks:
                 sc = banks.tile([P, BANK], F32, name="sc", tag="bank")
-                sc_ps.append(sc)
-                diagonal = c == n - 1
                 for ub in range(NB):
                     nc.tensor.matmul(
-                        sc[:, 0 : hi - lo],
-                        q_sb[:, ub, queries],
-                        k_sb[:, ub, lo:hi],
-                        start=(ub == 0),
-                        stop=(ub == NB - 1 and not diagonal),
+                        sc[:, 0 : hi - lo], q_sb[:, ub, queries], k_sb[:, ub, lo:hi], start=(ub == 0), stop=(ub == NB - 1)
                     )
                     bank = flip_next(steps, bank)
-                if diagonal:
-                    nc.tensor.matmul(sc[:, hi - lo - P : hi - lo], ident[:], mask[:], start=False, stop=True)
-                nc.vector.reduce_max(peak[:, c : c + 1], sc[:, 0 : hi - lo], axis=X)
+                if lo < width - P:
+                    pieces.append((sc[:, 0 : min(hi, width - P) - lo], lo, min(hi, width - P)))
+            diag = work.tile([P, P], F32, name="diag", tag="diag")
+            nc.vector.tensor_tensor(diag[:], sc[:, width - P - lo : width - lo], mask[:], ALU.add)
+            pieces.append((diag[:], width - P, width))
+            n = len(pieces)
+            for c, (scores, lo, hi) in enumerate(pieces):
+                nc.vector.reduce_max(peak[:, c : c + 1], scores, axis=X)
             negmax = small.tile([P, 1], F32, name="negmax", tag="negmax")
             nc.vector.reduce_max(negmax[:], peak[:, 0:n], axis=X, negate=True)
             ex = work.tile([P, T], F32, name="ex", tag="ex")
-            for c, (lo, hi) in enumerate(chunks):
+            for c, (scores, lo, hi) in enumerate(pieces):
                 nc.scalar.activation(
-                    ex[:, lo:hi], sc_ps[c][:, 0 : hi - lo], ACT.Exp, bias=negmax[:], scale=1.0, accum_out=part[:, c : c + 1]
+                    ex[:, lo:hi], scores, ACT.Exp, bias=negmax[:], scale=1.0, accum_out=part[:, c : c + 1]
                 )
             total = small.tile([P, 1], F32, name="total", tag="total")
             nc.vector.reduce_sum(total[:], part[:, 0:n], axis=X)

@@ -8,7 +8,6 @@ BANK = 512
 NB = T // P
 HALVES = T // BANK
 NEG = -1e30
-WARM = 6
 
 FLOPS = 2 * (2 * T * T * T + T * (T * (T + 1) // 2) + D * B * (T * (T + 1) // 2) + D * D * N)
 
@@ -54,12 +53,6 @@ def tile_lin_sfm_attention_b_kernel(tc, table, wv, pos, wq, wk, offs, out):
         nc.gpsimd.iota(ahead[:], pattern=[[1, P]], base=0, channel_multiplier=-1)
         mask = held.tile([P, P], BF16, name="mask")
         nc.vector.tensor_scalar(mask[:], ahead[:], 0.0, NEG, op0=ALU.is_gt, op1=ALU.mult)
-
-        zeros = held.tile([P, BANK], BF16, name="zeros")
-        nc.vector.memset(zeros[:], 0.0)
-        warm_ps = banks.tile([P, BANK], F32, name="warm_ps", tag="bank")
-        for n in range(WARM):
-            nc.tensor.matmul(warm_ps[:], zeros[:, 0:P], zeros[:], start=True, stop=True)
 
         v_sb = held.tile([P, N], BF16, name="v_sb")
         e_sb = held.tile([P, N], F32, name="e_sb")

@@ -27,20 +27,18 @@ def tile_lin_sfm_attention_b_kernel(tc, table, wv, pos, wq, wk, offs, out):
         tc.psum_pool(name="banks", bufs=6) as banks,
         tc.psum_pool(name="flipped", bufs=2) as flipped,
     ):
-        offsets = held.tile([P, N // 16], U16, name="offsets")
-        nc.sync.dma_start(offsets[:], offs)
         table_sb = held.tile([P, V], BF16, name="table_sb")
         nc.sync.dma_start(table_sb[:], table)
+        offsets = held.tile([P, N // 16], U16, name="offsets")
+        nc.sync.dma_start(offsets[:], offs)
         wv_sb = held.tile([P, D], BF16, name="wv_sb")
-        nc.scalar.dma_start(wv_sb[:], wv)
+        nc.sync.dma_start(wv_sb[:], wv)
         pos_sb = held.tile([P, NB, T], BF16, name="pos_sb")
         wk_sb = held.tile([P, NB, T], BF16, name="wk_sb")
         wq_sb = held.tile([P, NB, T], BF16, name="wq_sb")
 
         def load(dst, src, columns):
-            blocks = src.rearrange("(r p) c -> p r c", p=P)
-            nc.sync.dma_start(dst[:, 0 : NB // 2, columns], blocks[:, 0 : NB // 2, columns])
-            nc.scalar.dma_start(dst[:, NB // 2 : NB, columns], blocks[:, NB // 2 : NB, columns])
+            nc.sync.dma_start(dst[:, :, columns], src.rearrange("(r p) c -> p r c", p=P)[:, :, columns])
 
         load(pos_sb, pos, slice(0, BANK))
         load(wk_sb, wk, slice(0, T))

@@ -41,7 +41,8 @@ def tile_lin_sfm_attention_b_kernel(tc, table, wv, pos, wq, wk, offs, out):
             nc.sync.dma_start(dst[:, :, columns], src.rearrange("(r p) c -> p r c", p=P)[:, :, columns])
 
         load(pos_sb, pos, slice(0, BANK))
-        load(wk_sb, wk, slice(0, T))
+        load(wk_sb, wk, slice(0, BANK))
+        load(wk_sb, wk, slice(BANK, T))
         load(pos_sb, pos, slice(BANK, T))
         load(wq_sb, wq, slice(0, T))
 

@@ -27,23 +27,26 @@ def tile_lin_sfm_attention_b_kernel(tc, table, wv, pos, wq, wk, offs, out):
         tc.psum_pool(name="banks", bufs=6) as banks,
         tc.psum_pool(name="flipped", bufs=2) as flipped,
     ):
+        pos_sb = held.tile([P, NB, T], BF16, name="pos_sb")
+        wk_sb = held.tile([P, NB, T], BF16, name="wk_sb")
+        wq_sb = held.tile([P, NB, T], BF16, name="wq_sb")
+
+        def load(dst, src, columns, r_first=0, r_end=NB):
+            blocks = src.rearrange("(r p) c -> p r c", p=P)
+            nc.sync.dma_start(dst[:, r_first:r_end, columns], blocks[:, r_first:r_end, columns])
+
+        first_half, second_half = slice(0, BANK), slice(BANK, T)
+        for r_first, r_end in ((0, 1), (1, 2), (2, 4), (4, 8)):
+            load(pos_sb, pos, first_half, r_first, r_end)
+            load(wk_sb, wk, first_half, r_first, r_end)
+        load(wk_sb, wk, second_half)
         table_sb = held.tile([P, V], BF16, name="table_sb")
         nc.sync.dma_start(table_sb[:], table)
         offsets = held.tile([P, N // 16], U16, name="offsets")
         nc.sync.dma_start(offsets[:], offs)
         wv_sb = held.tile([P, D], BF16, name="wv_sb")
         nc.sync.dma_start(wv_sb[:], wv)
-        pos_sb = held.tile([P, NB, T], BF16, name="pos_sb")
-        wk_sb = held.tile([P, NB, T], BF16, name="wk_sb")
-        wq_sb = held.tile([P, NB, T], BF16, name="wq_sb")
-
-        def load(dst, src, columns):
-            nc.sync.dma_start(dst[:, :, columns], src.rearrange("(r p) c -> p r c", p=P)[:, :, columns])
-
-        load(pos_sb, pos, slice(0, BANK))
-        load(wk_sb, wk, slice(0, BANK))
-        load(wk_sb, wk, slice(BANK, T))
-        load(pos_sb, pos, slice(BANK, T))
+        load(pos_sb, pos, second_half)
         load(wq_sb, wq, slice(0, T))
 
         ident = held.tile([P, P], BF16, name="ident")
@@ -55,16 +58,18 @@ def tile_lin_sfm_attention_b_kernel(tc, table, wv, pos, wq, wk, offs, out):
 
         v_sb = held.tile([P, N], BF16, name="v_sb")
         e_sb = held.tile([P, N], F32, name="e_sb")
-        for j in range(0, N, BANK):
-            entries = slice(j, j + BANK)
-            piece = offsets[:, j // 16 : (j + BANK) // 16]
-            v_ps = banks.tile([P, BANK], F32, name="v_ps", tag="bank")
-            nc.tensor.matmul(v_ps[:], wv_sb[:], table_sb[:].indirect(piece), start=True, stop=True)
-            nc.vector.tensor_copy(v_sb[:, entries], v_ps[:])
-            e_ps = banks.tile([P, BANK], F32, name="e_ps", tag="bank")
-            nc.tensor.matmul(e_ps[:], ident[:], table_sb[:].indirect(piece), start=True, stop=True)
-            nc.scalar.activation(e_sb[:, entries], e_ps[:], ACT.Copy)
-            nc.sync.dma_start(out[D : 2 * D, entries], e_sb[:, entries])
+
+        def look_up():
+            for j in range(0, N, BANK):
+                entries = slice(j, j + BANK)
+                piece = offsets[:, j // 16 : (j + BANK) // 16]
+                v_ps = banks.tile([P, BANK], F32, name="v_ps", tag="bank")
+                nc.tensor.matmul(v_ps[:], wv_sb[:], table_sb[:].indirect(piece), start=True, stop=True)
+                nc.vector.tensor_copy(v_sb[:, entries], v_ps[:])
+                e_ps = banks.tile([P, BANK], F32, name="e_ps", tag="bank")
+                nc.tensor.matmul(e_ps[:], ident[:], table_sb[:].indirect(piece), start=True, stop=True)
+                nc.scalar.activation(e_sb[:, entries], e_ps[:], ACT.Copy)
+                nc.sync.dma_start(out[D : 2 * D, entries], e_sb[:, entries])
 
         vT_sb = held.tile([P, B * NB, P], BF16, name="vT_sb")
         aT_sb = held.tile([P, NB, T], BF16, name="aT_sb")
@@ -92,20 +97,22 @@ def tile_lin_sfm_attention_b_kernel(tc, table, wv, pos, wq, wk, offs, out):
         k_sb = held.tile([P, NB, T], BF16, name="k_sb")
         q_sb = held.tile([P, NB, T], BF16, name="q_sb")
 
-        def project(dst, w_sb, scale, h, guests):
+        def project(dst, w_sb, scale, h, guests, together=1):
             half = slice(h * BANK, (h + 1) * BANK)
             steps, bank = flip_steps(guests), None
-            for ub in range(NB):
-                acc = banks.tile([P, BANK], F32, name="acc", tag="bank")
+            for first in range(0, NB, together):
+                accs = [banks.tile([P, BANK], F32, name="acc", tag="bank") for ub in range(together)]
                 for r in range(NB):
-                    nc.tensor.matmul(
-                        acc[:], w_sb[:, r, ub * P : (ub + 1) * P], pos_sb[:, r, half], start=(r == 0), stop=(r == NB - 1)
-                    )
-                    bank = flip_next(steps, bank)
-                if ub % 2 == 0:
-                    nc.vector.tensor_scalar_mul(dst[:, ub, half], acc[:], scale)
-                else:
-                    nc.scalar.activation(dst[:, ub, half], acc[:], ACT.Copy, scale=scale)
+                    for ub, acc in enumerate(accs, first):
+                        nc.tensor.matmul(
+                            acc[:], w_sb[:, r, ub * P : (ub + 1) * P], pos_sb[:, r, half], start=(r == 0), stop=(r == NB - 1)
+                        )
+                        bank = flip_next(steps, bank)
+                for ub, acc in enumerate(accs, first):
+                    if ub % 2 == 0:
+                        nc.vector.tensor_scalar_mul(dst[:, ub, half], acc[:], scale)
+                    else:
+                        nc.scalar.activation(dst[:, ub, half], acc[:], ACT.Copy, scale=scale)
 
         def weights(i, guests):
             queries = slice(i * P, (i + 1) * P)
@@ -169,9 +176,10 @@ def tile_lin_sfm_attention_b_kernel(tc, table, wv, pos, wq, wk, offs, out):
             nc.sync.dma_start(out[0:D, entries], res_sb[:, entries])
 
         q_scale = 2.0 / T**0.5
-        project(k_sb, wk_sb, 1.0, 0, [v_guest(0)])
-        project(k_sb, wk_sb, 1.0, 1, [v_guest(1)])
-        project(q_sb, wq_sb, q_scale, 1, [v_guest(2)])
+        project(k_sb, wk_sb, 1.0, 0, [], together=NB // 2)
+        look_up()
+        project(k_sb, wk_sb, 1.0, 1, [v_guest(0)])
+        project(q_sb, wq_sb, q_scale, 1, [v_guest(1), v_guest(2)])
         a7 = weights(7, [])
         a6 = weights(6, [])
         a5 = weights(5, [])

@@ -49,6 +49,12 @@ def tile_lin_sfm_attention_b_kernel(tc, table, wv, pos, wq, wk, offs, out):
         load(pos_sb, pos, second_half)
         load(wq_sb, wq, slice(0, T))
 
+        zeros = held.tile([P, BANK], BF16, name="zeros")
+        nc.vector.memset(zeros[:], 0.0)
+        for warm_up in range(3):
+            idle = banks.tile([P, BANK], F32, name="idle", tag="bank")
+            nc.tensor.matmul(idle[:], zeros[:, 0:P], zeros[:], start=True, stop=True)
+
         ident = held.tile([P, P], BF16, name="ident")
         make_identity(nc, ident[:])
         ahead = held.tile([P, P], I32, name="ahead")

@@ -106,6 +106,8 @@ def tile_lin_sfm_attention_b_kernel(tc, table, wv, pos, wq, wk, offs, out):
         def project(dst, w_sb, scale, h, guests, together=1):
             half = slice(h * BANK, (h + 1) * BANK)
             steps, bank = flip_steps(guests), None
+            matmuls = 0
+            every = NB * NB // max(1, len(steps))
             for first in range(0, NB, together):
                 accs = [banks.tile([P, BANK], F32, name="acc", tag="bank") for ub in range(together)]
                 for r in range(NB):
@@ -113,28 +115,28 @@ def tile_lin_sfm_attention_b_kernel(tc, table, wv, pos, wq, wk, offs, out):
                         nc.tensor.matmul(
                             acc[:], w_sb[:, r, ub * P : (ub + 1) * P], pos_sb[:, r, half], start=(r == 0), stop=(r == NB - 1)
                         )
-                        bank = flip_next(steps, bank)
+                        matmuls += 1
+                        if matmuls % every == 0:
+                            bank = flip_next(steps, bank)
                 for ub, acc in enumerate(accs, first):
                     if ub % 2 == 0:
                         nc.vector.tensor_scalar_mul(dst[:, ub, half], acc[:], scale)
                     else:
                         nc.scalar.activation(dst[:, ub, half], acc[:], ACT.Copy, scale=scale)
 
-        def weights(i, guests):
+        def weights(i):
             queries = slice(i * P, (i + 1) * P)
             width = (i + 1) * P
             chunks = [(lo, min(lo + BANK, width)) for lo in range(0, width, BANK)]
             peak = small.tile([P, HALVES + 1], F32, name="peak", tag="peak")
             part = small.tile([P, HALVES + 1], F32, name="part", tag="part")
             pieces = []
-            steps, bank = flip_steps(guests), None
             for lo, hi in chunks:
                 sc = banks.tile([P, BANK], F32, name="sc", tag="bank")
                 for ub in range(NB):
                     nc.tensor.matmul(
                         sc[:, 0 : hi - lo], q_sb[:, ub, queries], k_sb[:, ub, lo:hi], start=(ub == 0), stop=(ub == NB - 1)
                     )
-                    bank = flip_next(steps, bank)
                 if lo < width - P:
                     pieces.append((sc[:, 0 : min(hi, width - P) - lo], lo, min(hi, width - P)))
             diag = work.tile([P, P], F32, name="diag", tag="diag")
@@ -184,17 +186,17 @@ def tile_lin_sfm_attention_b_kernel(tc, table, wv, pos, wq, wk, offs, out):
         q_scale = 2.0 / T**0.5
         project(k_sb, wk_sb, 1.0, 0, [], together=NB // 2)
         look_up()
-        project(k_sb, wk_sb, 1.0, 1, [v_guest(0)])
-        project(q_sb, wq_sb, q_scale, 1, [v_guest(1), v_guest(2)])
-        a7 = weights(7, [])
-        a6 = weights(6, [])
-        a5 = weights(5, [])
-        a4 = weights(4, [a_guest(7, a7)])
-        project(q_sb, wq_sb, q_scale, 0, [v_guest(3), a_guest(6, a6), a_guest(5, a5), a_guest(4, a4)])
-        a3 = weights(3, [])
-        a2 = weights(2, [])
-        a1 = weights(1, [])
-        a0 = weights(0, [])
+        project(k_sb, wk_sb, 1.0, 1, [v_guest(0), v_guest(1)])
+        project(q_sb, wq_sb, q_scale, 1, [v_guest(2), v_guest(3)])
+        a7 = weights(7)
+        a6 = weights(6)
+        a5 = weights(5)
+        a4 = weights(4)
+        project(q_sb, wq_sb, q_scale, 0, [a_guest(7, a7), a_guest(6, a6), a_guest(5, a5), a_guest(4, a4)])
+        a3 = weights(3)
+        a2 = weights(2)
+        a1 = weights(1)
+        a0 = weights(0)
         third, fourth = (2 * T // 4, 3 * T // 4), (3 * T // 4, T)
         mix(*third, 0, [])
         mix(*fourth, 0, [])

@@ -36,7 +36,10 @@ def tile_lin_sfm_attention_b_kernel(tc, table, wv, pos, wq, wk, offs, out):
             nc.sync.dma_start(dst[:, r_first:r_end, columns], blocks[:, r_first:r_end, columns])
 
         first_half, second_half = slice(0, BANK), slice(BANK, T)
-        for r_first, r_end in ((0, 1), (1, 2), (2, 4), (4, 8)):
+        load(wk_sb, wk, slice(0, P), 0, 1)
+        load(pos_sb, pos, first_half, 0, 1)
+        load(wk_sb, wk, slice(P, BANK), 0, 1)
+        for r_first, r_end in ((1, 2), (2, 4), (4, 6), (6, 8)):
             load(pos_sb, pos, first_half, r_first, r_end)
             load(wk_sb, wk, first_half, r_first, r_end)
         load(wk_sb, wk, second_half)

@@ -207,7 +207,7 @@ def tile_lin_sfm_attention_b_kernel(tc, table, wv, pos, wq, wk, offs, out):
         mix(*fourth, 1, [a_guest(2, a2)])
         mix(*third, 2, [a_guest(1, a1)])
         mix(*fourth, 2, [a_guest(0, a0)])
-        mix(*third, 3, [])
         for b in range(B):
             mix(0, BANK, b, [])
+        mix(*third, 3, [])
         mix(*fourth, 3, [])

@@ -60,10 +60,13 @@ def tile_lin_sfm_attention_b_kernel(tc, table, wv, pos, wq, wk, offs, out):
 
         ident = held.tile([P, P], BF16, name="ident")
         make_identity(nc, ident[:])
-        ahead = held.tile([P, P], I32, name="ahead")
-        nc.gpsimd.iota(ahead[:], pattern=[[1, P]], base=0, channel_multiplier=-1)
-        mask = held.tile([P, P], BF16, name="mask")
+        ahead = held.tile([P, BANK], I32, name="ahead")
+        nc.gpsimd.iota(ahead[:], pattern=[[1, BANK]], base=P - BANK, channel_multiplier=-1)
+        mask = held.tile([P, BANK], BF16, name="mask")
         nc.vector.tensor_scalar(mask[:], ahead[:], 0.0, NEG, op0=ALU.is_gt, op1=ALU.mult)
+        keep = held.tile([P, 1], F32, name="keep")
+        nc.vector.memset(keep[:], 1.0)
+        nc.vector.memset(keep[0:1, :], 0.0)
 
         v_sb = held.tile([P, N], BF16, name="v_sb")
         e_sb = held.tile([P, N], F32, name="e_sb")
@@ -131,8 +134,7 @@ def tile_lin_sfm_attention_b_kernel(tc, table, wv, pos, wq, wk, offs, out):
             queries = slice(i * P, (i + 1) * P)
             width = (i + 1) * P
             chunks = [(lo, min(lo + BANK, width)) for lo in range(0, width, BANK)]
-            peak = small.tile([P, HALVES + 1], F32, name="peak", tag="peak")
-            part = small.tile([P, HALVES + 1], F32, name="part", tag="part")
+            n = len(chunks)
             pieces = []
             for lo, hi in chunks:
                 sc = banks.tile([P, BANK], F32, name="sc", tag="bank")
@@ -140,29 +142,34 @@ def tile_lin_sfm_attention_b_kernel(tc, table, wv, pos, wq, wk, offs, out):
                     nc.tensor.matmul(
                         sc[:, 0 : hi - lo], q_sb[:, ub, queries], k_sb[:, ub, lo:hi], start=(ub == 0), stop=(ub == NB - 1)
                     )
-                if lo < width - P:
-                    pieces.append((sc[:, 0 : min(hi, width - P) - lo], lo, min(hi, width - P)))
-            diag = work.tile([P, P], F32, name="diag", tag="diag")
-            nc.vector.tensor_tensor(diag[:], sc[:, width - P - lo : width - lo], mask[:], ALU.add)
-            pieces.append((diag[:], width - P, width))
-            n = len(pieces)
-            for c, (scores, lo, hi) in enumerate(pieces):
-                nc.vector.reduce_max(peak[:, c : c + 1], scores, axis=X)
+                pieces.append(sc[:, 0 : hi - lo])
+            masked = work.tile([P, BANK], F32, name="masked", tag="masked")
+            nc.vector.tensor_tensor(masked[:, 0 : hi - lo], sc[:, 0 : hi - lo], mask[:, BANK - (hi - lo) : BANK], ALU.add)
+            pieces[-1] = masked[:, 0 : hi - lo]
             negmax = small.tile([P, 1], F32, name="negmax", tag="negmax")
-            nc.vector.reduce_max(negmax[:], peak[:, 0:n], axis=X, negate=True)
-            ex = work.tile([P, T], F32, name="ex", tag="ex")
-            for c, (scores, lo, hi) in enumerate(pieces):
-                nc.scalar.activation(
-                    ex[:, lo:hi], scores, ACT.Exp, bias=negmax[:], scale=1.0, accum_out=part[:, c : c + 1]
-                )
             total = small.tile([P, 1], F32, name="total", tag="total")
-            nc.vector.reduce_sum(total[:], part[:, 0:n], axis=X)
+            ex = work.tile([P, T], F32, name="ex", tag="ex")
+            if n == 1:
+                nc.vector.reduce_max(negmax[:], pieces[0], axis=X, negate=True)
+                nc.scalar.activation(ex[:, 0:width], pieces[0], ACT.Exp, bias=negmax[:], scale=1.0, accum_out=total[:])
+            else:
+                peak = small.tile([P, HALVES], F32, name="peak", tag="peak")
+                part = small.tile([P, HALVES], F32, name="part", tag="part")
+                for c in range(n):
+                    nc.vector.reduce_max(peak[:, c : c + 1], pieces[c], axis=X)
+                nc.vector.reduce_max(negmax[:], peak[:, 0:n], axis=X, negate=True)
+                for c, (lo, hi) in enumerate(chunks):
+                    nc.scalar.activation(
+                        ex[:, lo:hi], pieces[c], ACT.Exp, bias=negmax[:], scale=1.0, accum_out=part[:, c : c + 1]
+                    )
+                nc.vector.reduce_sum(total[:], part[:, 0:n], axis=X)
             rsum = small.tile([P, 1], F32, name="rsum", tag="rsum")
             nc.vector.reciprocal(rsum[:], total[:])
-            if i == 0:
-                nc.vector.memset(rsum[0:1, :], 0.0)
             a = unflipped.tile([P, T], BF16, name="a", tag="a")
-            nc.vector.tensor_scalar_mul(a[:, 0:width], ex[:, 0:width], rsum[:])
+            if i == 0:
+                nc.vector.tensor_scalar(a[:, 0:width], ex[:, 0:width], rsum[:], keep[:], op0=ALU.mult, op1=ALU.mult)
+            else:
+                nc.vector.tensor_scalar_mul(a[:, 0:width], ex[:, 0:width], rsum[:])
             return a
 
         res_sb = held.tile([P, N], F32, name="res_sb")

@@ -207,14 +207,16 @@ def tile_lin_sfm_attention_b_kernel(tc, table, wv, pos, wq, wk, offs, out):
         a2 = weights(2)
         a1 = weights(1)
         a0 = weights(0)
-        third, fourth = (2 * T // 4, 3 * T // 4), (3 * T // 4, T)
+        early, second, third, fourth = [(lo, lo + T // 4) for lo in range(0, T, T // 4)]
         mix(*third, 0, [])
         mix(*fourth, 0, [])
-        mix(*third, 1, [a_guest(3, a3)])
-        mix(*fourth, 1, [a_guest(2, a2)])
-        mix(*third, 2, [a_guest(1, a1)])
-        mix(*fourth, 2, [a_guest(0, a0)])
-        for b in range(B):
+        mix(*third, 1, [])
+        mix(*fourth, 1, [a_guest(3, a3)])
+        mix(*third, 2, [a_guest(2, a2)])
+        mix(*fourth, 2, [a_guest(1, a1)])
+        mix(*third, 3, [a_guest(0, a0)])
+        mix(*second, 0, [])
+        mix(*early, 0, [])
+        for b in range(1, B):
             mix(0, BANK, b, [])
-        mix(*third, 3, [])
         mix(*fourth, 3, [])

import concourse.mybir as mybir
from concourse.masks import make_identity

P = 128
D, V, T, B = 128, 2048, 1024, 4
N = B * T
BANK = 512
NB = T // P
HALVES = T // BANK
NEG = -1e30

FLOPS = 2 * (2 * T * T * T + T * (T * (T + 1) // 2) + D * B * (T * (T + 1) // 2) + D * D * N)

BF16, F32, U16, I32 = mybir.dt.bfloat16, mybir.dt.float32, mybir.dt.uint16, mybir.dt.int32
ACT = mybir.ActivationFunctionType
ALU = mybir.AluOpType
X = mybir.AxisListType.X


def tile_lin_sfm_attention_b_kernel(tc, table, wv, pos, wq, wk, offs, out):
    nc = tc.nc
    with (
        tc.tile_pool(name="held", bufs=1) as held,
        tc.tile_pool(name="work", bufs=2) as work,
        tc.tile_pool(name="unflipped", bufs=4) as unflipped,
        tc.tile_pool(name="small", bufs=2) as small,
        tc.psum_pool(name="banks", bufs=6) as banks,
        tc.psum_pool(name="flipped", bufs=2) as flipped,
    ):
        pos_sb = held.tile([P, NB, T], BF16, name="pos_sb")
        wk_sb = held.tile([P, NB, T], BF16, name="wk_sb")
        wq_sb = held.tile([P, NB, T], BF16, name="wq_sb")

        def load(dst, src, columns, r_first=0, r_end=NB):
            blocks = src.rearrange("(r p) c -> p r c", p=P)
            nc.sync.dma_start(dst[:, r_first:r_end, columns], blocks[:, r_first:r_end, columns])

        first_half, second_half = slice(0, BANK), slice(BANK, T)
        load(wk_sb, wk, slice(0, P), 0, 1)
        load(pos_sb, pos, first_half, 0, 1)
        load(wk_sb, wk, slice(P, BANK), 0, 1)
        for r_first, r_end in ((1, 2), (2, 4), (4, 6), (6, 8)):
            load(pos_sb, pos, first_half, r_first, r_end)
            load(wk_sb, wk, first_half, r_first, r_end)
        load(wk_sb, wk, second_half)
        table_sb = held.tile([P, V], BF16, name="table_sb")
        nc.sync.dma_start(table_sb[:], table)
        offsets = held.tile([P, N // 16], U16, name="offsets")
        nc.sync.dma_start(offsets[:], offs)
        wv_sb = held.tile([P, D], BF16, name="wv_sb")
        nc.sync.dma_start(wv_sb[:], wv)
        load(pos_sb, pos, second_half)
        load(wq_sb, wq, slice(0, T))

        zeros = held.tile([P, BANK], BF16, name="zeros")
        nc.vector.memset(zeros[:], 0.0)
        for warm_up in range(3):
            idle = banks.tile([P, BANK], F32, name="idle", tag="bank")
            nc.tensor.matmul(idle[:], zeros[:, 0:P], zeros[:], start=True, stop=True)

        ident = held.tile([P, P], BF16, name="ident")
        make_identity(nc, ident[:])
        ahead = held.tile([P, BANK], I32, name="ahead")
        nc.gpsimd.iota(ahead[:], pattern=[[1, BANK]], base=P - BANK, channel_multiplier=-1)
        mask = held.tile([P, BANK], BF16, name="mask")
        nc.vector.tensor_scalar(mask[:], ahead[:], 0.0, NEG, op0=ALU.is_gt, op1=ALU.mult)
        keep = held.tile([P, 1], F32, name="keep")
        nc.vector.memset(keep[:], 1.0)
        nc.vector.memset(keep[0:1, :], 0.0)

        v_sb = held.tile([P, N], BF16, name="v_sb")
        e_sb = held.tile([P, N], F32, name="e_sb")

        def look_up():
            for j in range(0, N, BANK):
                entries = slice(j, j + BANK)
                piece = offsets[:, j // 16 : (j + BANK) // 16]
                v_ps = banks.tile([P, BANK], F32, name="v_ps", tag="bank")
                nc.tensor.matmul(v_ps[:], wv_sb[:], table_sb[:].indirect(piece), start=True, stop=True)
                nc.vector.tensor_copy(v_sb[:, entries], v_ps[:])
                e_ps = banks.tile([P, BANK], F32, name="e_ps", tag="bank")
                nc.tensor.matmul(e_ps[:], ident[:], table_sb[:].indirect(piece), start=True, stop=True)
                nc.scalar.activation(e_sb[:, entries], e_ps[:], ACT.Copy)
                nc.sync.dma_start(out[D : 2 * D, entries], e_sb[:, entries])

        vT_sb = held.tile([P, B * NB, P], BF16, name="vT_sb")
        aT_sb = held.tile([P, NB, T], BF16, name="aT_sb")

        def flip_steps(guests):
            return [(src, n, blocks, dst) for src, blocks, dst in guests for n in range(blocks)]

        def flip_next(steps, bank):
            if not steps:
                return bank
            src, n, blocks, dst = steps.pop(0)
            if n == 0:
                bank = flipped.tile([P, T], BF16, name="bank", tag="flip")
            nc.tensor.transpose(bank[:, n * P : (n + 1) * P], src[:, n * P : (n + 1) * P], ident[:])
            if n == blocks - 1:
                nc.scalar.activation(dst, bank[:, 0 : blocks * P].rearrange("p (n c) -> p n c", c=P), ACT.Copy)
            return bank

        def v_guest(b):
            return (v_sb[:, b * T : (b + 1) * T], NB, vT_sb[:, b * NB : (b + 1) * NB, :])

        def a_guest(g, a_g):
            return (a_g, g + 1, aT_sb[:, 0 : g + 1, g * P : (g + 1) * P])

        k_sb = held.tile([P, NB, T], BF16, name="k_sb")
        q_sb = held.tile([P, NB, T], BF16, name="q_sb")

        def project(dst, w_sb, scale, h, guests, together=1):
            half = slice(h * BANK, (h + 1) * BANK)
            steps, bank = flip_steps(guests), None
            matmuls = 0
            every = NB * NB // max(1, len(steps))
            for first in range(0, NB, together):
                accs = [banks.tile([P, BANK], F32, name="acc", tag="bank") for ub in range(together)]
                for r in range(NB):
                    for ub, acc in enumerate(accs, first):
                        nc.tensor.matmul(
                            acc[:], w_sb[:, r, ub * P : (ub + 1) * P], pos_sb[:, r, half], start=(r == 0), stop=(r == NB - 1)
                        )
                        matmuls += 1
                        if matmuls % every == 0:
                            bank = flip_next(steps, bank)
                for ub, acc in enumerate(accs, first):
                    if ub % 2 == 0:
                        nc.vector.tensor_scalar_mul(dst[:, ub, half], acc[:], scale)
                    else:
                        nc.scalar.activation(dst[:, ub, half], acc[:], ACT.Copy, scale=scale)

        def weights(i):
            queries = slice(i * P, (i + 1) * P)
            width = (i + 1) * P
            chunks = [(lo, min(lo + BANK, width)) for lo in range(0, width, BANK)]
            n = len(chunks)
            pieces = []
            for lo, hi in chunks:
                sc = banks.tile([P, BANK], F32, name="sc", tag="bank")
                for ub in range(NB):
                    nc.tensor.matmul(
                        sc[:, 0 : hi - lo], q_sb[:, ub, queries], k_sb[:, ub, lo:hi], start=(ub == 0), stop=(ub == NB - 1)
                    )
                pieces.append(sc[:, 0 : hi - lo])
            masked = work.tile([P, BANK], F32, name="masked", tag="masked")
            nc.vector.tensor_tensor(masked[:, 0 : hi - lo], sc[:, 0 : hi - lo], mask[:, BANK - (hi - lo) : BANK], ALU.add)
            pieces[-1] = masked[:, 0 : hi - lo]
            negmax = small.tile([P, 1], F32, name="negmax", tag="negmax")
            total = small.tile([P, 1], F32, name="total", tag="total")
            ex = work.tile([P, T], F32, name="ex", tag="ex")
            if n == 1:
                nc.vector.reduce_max(negmax[:], pieces[0], axis=X, negate=True)
                nc.scalar.activation(ex[:, 0:width], pieces[0], ACT.Exp, bias=negmax[:], scale=1.0, accum_out=total[:])
            else:
                peak = small.tile([P, HALVES], F32, name="peak", tag="peak")
                part = small.tile([P, HALVES], F32, name="part", tag="part")
                for c in range(n):
                    nc.vector.reduce_max(peak[:, c : c + 1], pieces[c], axis=X)
                nc.vector.reduce_max(negmax[:], peak[:, 0:n], axis=X, negate=True)
                for c, (lo, hi) in enumerate(chunks):
                    nc.scalar.activation(
                        ex[:, lo:hi], pieces[c], ACT.Exp, bias=negmax[:], scale=1.0, accum_out=part[:, c : c + 1]
                    )
                nc.vector.reduce_sum(total[:], part[:, 0:n], axis=X)
            rsum = small.tile([P, 1], F32, name="rsum", tag="rsum")
            nc.vector.reciprocal(rsum[:], total[:])
            a = unflipped.tile([P, T], BF16, name="a", tag="a")
            if i == 0:
                nc.vector.tensor_scalar(a[:, 0:width], ex[:, 0:width], rsum[:], keep[:], op0=ALU.mult, op1=ALU.mult)
            else:
                nc.vector.tensor_scalar_mul(a[:, 0:width], ex[:, 0:width], rsum[:])
            return a

        res_sb = held.tile([P, N], F32, name="res_sb")

        def mix(s_first, s_end, b, guests):
            width = s_end - s_first
            last_tb = s_end // P - 1
            y_ps = banks.tile([P, BANK], F32, name="y_ps", tag="bank")
            steps, bank = flip_steps(guests), None
            for tb in range(last_tb + 1):
                s_from = max(tb * P, s_first)
                nc.tensor.matmul(
                    y_ps[:, s_from - s_first : width],
                    vT_sb[:, b * NB + tb, :],
                    aT_sb[:, tb, s_from:s_end],
                    start=(tb == 0),
                    stop=(tb == last_tb),
                )
                bank = flip_next(steps, bank)
            entries = slice(b * T + s_first, b * T + s_end)
            nc.vector.tensor_tensor(res_sb[:, entries], y_ps[:, 0:width], e_sb[:, entries], ALU.add)
            nc.sync.dma_start(out[0:D, entries], res_sb[:, entries])

        q_scale = 2.0 / T**0.5
        project(k_sb, wk_sb, 1.0, 0, [], together=NB // 2)
        look_up()
        project(k_sb, wk_sb, 1.0, 1, [v_guest(0), v_guest(1)])
        project(q_sb, wq_sb, q_scale, 1, [v_guest(2), v_guest(3)])
        a7 = weights(7)
        a6 = weights(6)
        a5 = weights(5)
        a4 = weights(4)
        project(q_sb, wq_sb, q_scale, 0, [a_guest(7, a7), a_guest(6, a6), a_guest(5, a5), a_guest(4, a4)])
        a3 = weights(3)
        a2 = weights(2)
        a1 = weights(1)
        a0 = weights(0)
        early, second, third, fourth = [(lo, lo + T // 4) for lo in range(0, T, T // 4)]
        mix(*third, 0, [])
        mix(*fourth, 0, [])
        mix(*third, 1, [])
        mix(*fourth, 1, [a_guest(3, a3)])
        mix(*third, 2, [a_guest(2, a2)])
        mix(*fourth, 2, [a_guest(1, a1)])
        mix(*third, 3, [a_guest(0, a0)])
        mix(*second, 0, [])
        mix(*early, 0, [])
        for b in range(1, B):
            mix(0, BANK, b, [])
        mix(*fourth, 3, [])
